import numpy as np
import ml_dtypes


def mxq(x, axis, fmt="e4m3"):
    dtype, down = {"e4m3": (ml_dtypes.float8_e4m3fn, 7), "e5m2": (ml_dtypes.float8_e5m2, 14)}[fmt]
    v = np.moveaxis(np.asarray(x, np.float32).astype(ml_dtypes.bfloat16).astype(np.float64), axis, -1)
    blocks = v.reshape(v.shape[:-1] + (-1, 32))
    amax = np.abs(blocks).max(-1, keepdims=True)
    byte = np.maximum(np.where(amax > 0, np.frexp(amax)[1] - 1 + 127, 0) - down, 1)
    scale = np.exp2(byte - 127.0)
    codes = (blocks / scale).astype(np.float32).astype(dtype).astype(np.float64)
    return np.moveaxis((codes * scale).reshape(v.shape), -1, axis)


WIDE = False


def mx_kscale(k):
    if not WIDE:
        return np.ones(k)
    levels = np.array([10, -10, 5, -5, 0])
    if k % 512:
        return np.exp2(np.random.permutation(np.resize(levels, k // 32))).repeat(32)
    a = np.empty((k // 512, 16))
    for p in range(k // 512):
        a[p, :8] = np.random.permutation(np.resize(levels, 8))
        for g in range(8):
            far = levels[np.abs(levels - a[p, g]) >= 10]
            a[p, g + 8] = far[np.random.randint(len(far))]
    return np.exp2(a.ravel()).repeat(32)


BF16 = ml_dtypes.bfloat16


def bf(x):
    return np.asarray(x, np.float32).astype(BF16)


def f64(x):
    return np.asarray(x).astype(np.float64)


B, K, N = 2048, 512, 1024


def setup_inputs():
    s = mx_kscale(B)[:, None]
    u = mx_kscale(N)
    x0 = bf(np.random.standard_normal((B, K)))
    W0 = bf(np.random.standard_normal((K, N)) * 0.4 / np.sqrt(K))
    P = bf(np.random.standard_normal(N) * 0.3)
    w = bf(0.8 + 0.1 * np.random.standard_normal(1))
    p = bf(0.5 + 0.1 * np.random.standard_normal(1))
    sine_w = bf(1.2 + 0.1 * np.random.standard_normal(1))
    cosine_w = bf(-0.7 + 0.1 * np.random.standard_normal(1))
    fac = np.concatenate((np.ones(K), u))
    g = bf(np.random.standard_normal((B, K + N)) * np.exp2(np.random.randint(-6, 1, (B, 1))) * 4.0 / s * fac)
    z = f64(x0) @ f64(W0) + f64(P)
    return {"x": bf(f64(x0) * s), "W": bf(f64(W0) / u), "P": P, "w": w, "p": p,
            "sine_w": sine_w, "cosine_w": cosine_w,
            "z": np.asarray(z, np.float32), "grad_out": g}


def reference(x, W, P, w, p, sine_w, cosine_w, z, grad_out):
    g = f64(grad_out)
    g1 = g[:, :K]
    g2 = g[:, K:]
    zf = f64(z)
    dz = g2 * (f64(sine_w) * np.cos(zf) - f64(cosine_w) * np.sin(zf))
    dx = f64(w) * g1 + (mxq(dz, 1, "e5m2") @ mxq(f64(W), 1, "e4m3").T)
    dW = mxq(f64(x), 0, "e4m3").T @ mxq(dz, 0, "e5m2")
    return dx, dW

@@ -1,0 +1,337 @@
+from contextlib import ExitStack
+
+import concourse.mybir as mybir
+from concourse.masks import make_identity
+
+FLOPS = 2 * 2 * 2048 * 1024 * 512
+
+F32 = mybir.dt.float32
+BF16 = mybir.dt.bfloat16
+I32 = mybir.dt.int32
+U32 = mybir.dt.uint32
+U8 = mybir.dt.uint8
+E4 = mybir.dt.float8_e4m3fn_x4
+E5 = mybir.dt.float8_e5m2_x4
+ALU = mybir.AluOpType
+ACT = mybir.ActivationFunctionType
+
+P = 128
+J = 4
+PASS = 512
+G = 4
+H = 2
+NCH = G * H
+HALF = 1024
+PI = 3.141592653589793
+TWO_PI = 2.0 * PI
+
+
+def tile_time2vec_t_v_kernel(tc, x, W, P_vec, w, p_sc, sine_w, cosine_w, z, grad_out, out_0, out_1):
+    nc = tc.nc
+
+    z_v = z.rearrange("(g p j) f -> g p j f", p=P, j=J)
+    go_v = grad_out.rearrange("(g p j) c -> g p j c", p=P, j=J)
+    x_v = x.rearrange("(g p j) f -> g p j f", p=P, j=J)
+    w_v = W.rearrange("(a p) n -> p a n", p=P)
+    o0_v = out_0.rearrange("(g p j) k -> g p j k", p=P, j=J)
+
+    with ExitStack() as ctx:
+        const = ctx.enter_context(tc.tile_pool(name="const", bufs=1))
+        keep = ctx.enter_context(tc.tile_pool(name="keep", bufs=1))
+        stream = ctx.enter_context(tc.tile_pool(name="stream", bufs=2))
+        psum = ctx.enter_context(tc.psum_pool(name="psum", bufs=1))
+        ctx.enter_context(tc.manual_schedule())
+
+        def small(name, cols=1, dtype=F32):
+            return const.tile([P, cols], dtype, name=name, tag=name)
+
+        swb = small("swb", 1, BF16)
+        cwb = small("cwb", 1, BF16)
+        wb = small("wb", 1, BF16)
+        with nc.allow_non_contiguous_dma(reason="one scalar spread over the partitions"):
+            nc.sync.dma_start(out=swb[:], in_=sine_w.partition_broadcast(P))
+            nc.scalar.dma_start(out=cwb[:], in_=cosine_w.partition_broadcast(P))
+            nc.gpsimd.dma_start(out=wb[:], in_=w.partition_broadcast(P))
+
+        warm = small("warm")
+        nc.vector.memset(warm[:], 0.0)
+        warm2 = small("warm2")
+        nc.scalar.activation(out=warm2[:], in_=warm[:], func=ACT.Sin)
+        ident = const.tile([P, P], F32, name="ident", tag="ident")
+        make_identity(nc, ident[:])
+
+        x_sb = []
+        for g in range(G):
+            xt = keep.tile([P, J, PASS], BF16, name="x%d" % g, tag="x%d" % g)
+            nc.sync.dma_start(out=xt[:], in_=x_v[g])
+            x_sb.append(xt)
+
+        z_sb = {}
+        g2_sb = {}
+        g1_sb = {}
+
+        def load_chunk(c):
+            h, g = divmod(c, G)
+            zt = stream.tile([P, J, PASS], F32, name="z%d" % c, tag="z", bufs=4)
+            nc.sync.dma_start(out=zt[:], in_=z_v[g][:, :, h * PASS:(h + 1) * PASS])
+            gt = stream.tile([P, J, PASS], BF16, name="g2_%d" % c, tag="g2", bufs=4)
+            nc.sync.dma_start(out=gt[:], in_=go_v[g][:, :, PASS * (1 + h):PASS * (2 + h)])
+            z_sb[c] = zt
+            g2_sb[c] = gt
+
+        def load_g1(g):
+            gt = keep.tile([P, J, PASS], BF16, name="g1_%d" % g, tag="g1_%d" % g)
+            nc.sync.dma_start(out=gt[:], in_=go_v[g][:, :, 0:PASS])
+            g1_sb[g] = gt
+
+        load_chunk(0)
+        w_sb = keep.tile([P, 4, 2 * PASS], BF16, name="w_sb", tag="w_sb")
+        nc.sync.dma_start(out=w_sb[:], in_=w_v)
+        load_chunk(1)
+        load_chunk(2)
+
+        sw2 = small("sw2")
+        cw2 = small("cw2")
+        pr = small("pr")
+        nc.vector.tensor_tensor(out=sw2[:], in0=swb[:], in1=swb[:], op=ALU.mult)
+        nc.vector.tensor_tensor(out=cw2[:], in0=cwb[:], in1=cwb[:], op=ALU.mult)
+        nc.vector.tensor_tensor(out=pr[:], in0=swb[:], in1=cwb[:], op=ALU.mult)
+        n2 = small("n2")
+        df = small("df")
+        nc.vector.tensor_tensor(out=n2[:], in0=sw2[:], in1=cw2[:], op=ALU.add)
+        nc.vector.tensor_tensor(out=df[:], in0=cw2[:], in1=sw2[:], op=ALU.subtract)
+        n2c = small("n2c")
+        nc.vector.tensor_scalar_max(out=n2c[:], in0=n2[:], scalar1=1e-30)
+        two_or_0 = small("two_or_0")
+        nc.vector.tensor_scalar(out=two_or_0[:], in0=df[:], scalar1=0.0, scalar2=2.0, op0=ALU.is_ge, op1=ALU.mult)
+        inv = small("inv")
+        nc.vector.reciprocal(out=inv[:], in_=n2c[:])
+        q = small("q")
+        nc.vector.tensor_scalar(out=q[:], in0=two_or_0[:], scalar1=1.0, scalar2=inv[:, 0:1],
+                                op0=ALU.subtract, op1=ALU.mult)
+        s2 = small("s2")
+        nc.vector.tensor_scalar(out=s2[:], in0=pr[:], scalar1=q[:, 0:1], scalar2=-2.0, op0=ALU.mult, op1=ALU.mult)
+        nc2 = small("nc2")
+        nc.vector.tensor_scalar(out=nc2[:], in0=df[:], scalar1=q[:, 0:1], scalar2=-1.0, op0=ALU.mult, op1=ALU.mult)
+        pair = small("pair", 2)
+        nc.vector.tensor_copy(out=pair[:, 0:1], in_=s2[:])
+        nc.vector.tensor_scalar_add(out=pair[:, 1:2], in0=s2[:], scalar1=0.5 * PI)
+        off = small("off")
+        nc.vector.tensor_scalar(out=off[:], in0=two_or_0[:], scalar1=-0.25 * PI, scalar2=0.5 * PI,
+                                op0=ALU.mult, op1=ALU.add)
+        swf = small("swf")
+        ncw = small("ncw")
+        wf = small("wf")
+        nc.vector.tensor_copy(out=swf[:], in_=swb[:])
+        nc.vector.tensor_scalar_mul(out=ncw[:], in0=cwb[:], scalar1=-1.0)
+
+        sc = small("sc", 2)
+        mm = small("mm")
+        dd = small("dd")
+        for it in range(3):
+            nc.scalar.activation(out=sc[:], in_=pair[:], func=ACT.Sin)
+            nc.scalar.activation(out=mm[:], in_=sc[:, 1:2], func=ACT.Copy, scale=s2[:, 0:1])
+            nc.scalar.activation(out=dd[:], in_=sc[:, 0:1], func=ACT.Identity, scale=nc2[:, 0:1], bias=mm[:, 0:1])
+            nc.scalar.activation(out=pair[:], in_=pair[:], func=ACT.Identity, scale=1.0, bias=dd[:, 0:1])
+        phi = small("phi")
+        nc.scalar.activation(out=phi[:], in_=pair[:, 0:1], func=ACT.Identity, scale=0.5, bias=off[:, 0:1])
+        turns = small("turns")
+        nc.scalar.activation(out=turns[:], in_=phi[:], func=ACT.Copy, scale=1.0 / TWO_PI)
+
+        xc = keep.tile([P, G, PASS], U32, name="xc", tag="xc", align_bytes=64)
+        xs = keep.tile([P, G, PASS], U8, name="xs", tag="xs", align_bytes=64)
+        xg_t = {}
+
+        def x_interleave(g, on_vector):
+            xg = stream.tile([P, PASS, J], BF16, name="xg%d" % g, tag="xg", bufs=2, align_bytes=64)
+            if on_vector:
+                nc.vector.tensor_copy(out=xg[:], in_=x_sb[g][:].rearrange("p j f -> p f j"))
+            else:
+                nc.scalar.copy(out=xg[:], in_=x_sb[g][:].rearrange("p j f -> p f j"))
+            xg_t[g] = xg
+
+        def x_quantize(g):
+            nc.vector.quantize_mx(out=xc[:, g, :].bitcast(E4), scales=xs[:, g, :],
+                                  in_=xg_t[g][:].rearrange("p f j -> p (f j)"))
+
+        x_interleave(0, True)
+        x_interleave(1, True)
+        x_quantize(0)
+        x_interleave(2, True)
+        x_quantize(1)
+        nc.vector.tensor_copy(out=wf[:], in_=wb[:])
+        x_quantize(2)
+
+        pa = small("pa", 2)
+        nc.vector.tensor_copy(out=pa[:, 0:1], in_=phi[:])
+        nc.vector.tensor_scalar(out=pa[:, 1:2], in0=phi[:], scalar1=-1.0, scalar2=0.5 * PI, op0=ALU.mult, op1=ALU.add)
+        sc2 = small("sc2", 2)
+        nc.scalar.activation(out=sc2[:], in_=pa[:], func=ACT.Sin)
+        m2 = small("m2")
+        nc.scalar.activation(out=m2[:], in_=sc2[:, 0:1], func=ACT.Copy, scale=swf[:, 0:1])
+        amp = small("amp")
+        nc.scalar.activation(out=amp[:], in_=sc2[:, 1:2], func=ACT.Identity, scale=ncw[:, 0:1], bias=m2[:, 0:1])
+
+        wc = keep.tile([P, H, PASS], U32, name="wc", tag="wc", align_bytes=64)
+        ws = keep.tile([P, H, PASS], U8, name="ws", tag="ws", align_bytes=64)
+        w_words = w_sb[:].rearrange("p a n -> p (a n)").bitcast(F32)
+        wg_t = {}
+
+        def w_turn(h):
+            wg = stream.tile([P, PASS, J], BF16, name="wg%d" % h, tag="wg", bufs=2, align_bytes=64)
+            wg_words = wg[:].rearrange("q c t -> q (c t)").bitcast(F32)
+            wg_t[h] = wg
+            for ap in range(2):
+                tp = psum.tile([P, 2, 2, P], F32, name="tpw%d%d" % (h, ap), tag="tp", bufs=2)
+                for l in range(2):
+                    base = (2 * ap + l) * PASS + 256 * h
+                    for u in range(2):
+                        nc.tensor.transpose(tp[:, l, u, :], w_words[:, base + u:base + 256:2], ident[:])
+                nc.scalar.copy(
+                    out=wg_words[:, ap * PASS:(ap + 1) * PASS].rearrange("q (l p u) -> q l p u", l=2, u=2),
+                    in_=tp[:].rearrange("q l u p -> q l p u"))
+
+        def w_quantize(h):
+            nc.vector.quantize_mx(out=wc[:, h, :].bitcast(E4), scales=ws[:, h, :],
+                                  in_=wg_t[h][:].rearrange("q c t -> q (c t)"))
+
+        fc = keep.tile([P, NCH, PASS], U32, name="fc", tag="fc", align_bytes=64)
+        fs = keep.tile([P, NCH, PASS], U8, name="fs", tag="fs", align_bytes=64)
+        dz_t = {}
+        dzg_t = {}
+        fg_t = {}
+        tc_t = {}
+        ts_t = {}
+        acc1 = {}
+        acc0 = {}
+        o0_t = {}
+
+        def reduce_range(c):
+            zf = z_sb[c][:].rearrange("p j f -> p (j f)")
+            kt = stream.tile([P, J * PASS], I32, name="k%d" % c, tag="k", bufs=2)
+            for a in range(2):
+                cols = slice(a * HALF, (a + 1) * HALF)
+                nc.vector.tensor_scalar(out=kt[:, cols], in0=zf[:, cols], scalar1=1.0 / TWO_PI,
+                                        scalar2=turns[:, 0:1], op0=ALU.mult, op1=ALU.add)
+            for a in range(2):
+                cols = slice(a * HALF, (a + 1) * HALF)
+                nc.vector.scalar_tensor_tensor(out=zf[:, cols], in0=kt[:, cols], scalar=-TWO_PI, in1=zf[:, cols],
+                                               op0=ALU.mult, op1=ALU.add)
+
+        def sine(c):
+            zf = z_sb[c][:].rearrange("p j f -> p (j f)")
+            for a in range(2):
+                cols = slice(a * HALF, (a + 1) * HALF)
+                nc.scalar.activation(out=zf[:, cols], in_=zf[:, cols], func=ACT.Sin, bias=phi[:, 0:1], scale=1.0)
+
+        def make_dz(c):
+            zf = z_sb[c][:].rearrange("p j f -> p (j f)")
+            gf = g2_sb[c][:].rearrange("p j f -> p (j f)")
+            dz = stream.tile([P, J, PASS], BF16, name="dz%d" % c, tag="dz", bufs=3)
+            dzf = dz[:].rearrange("p j f -> p (j f)")
+            for a in range(2):
+                cols = slice(a * HALF, (a + 1) * HALF)
+                nc.vector.scalar_tensor_tensor(out=dzf[:, cols], in0=zf[:, cols], scalar=amp[:, 0:1],
+                                               in1=gf[:, cols], op0=ALU.mult, op1=ALU.mult)
+            dz_t[c] = dz
+
+        def turn(c):
+            dz = dz_t[c]
+            words = dz[:].rearrange("p j f -> p (j f)").bitcast(F32)
+            tps = []
+            for jp in range(2):
+                tp = psum.tile([P, 2, 2, P], F32, name="tp%d_%d" % (c, jp), tag="tp", bufs=2)
+                for l in range(2):
+                    base = (2 * jp + l) * 256
+                    for u in range(2):
+                        nc.tensor.transpose(tp[:, l, u, :], words[:, base + u:base + 256:2], ident[:])
+                tps.append(tp)
+            dzg = stream.tile([P, PASS, J], BF16, name="dzg%d" % c, tag="dzg", bufs=2, align_bytes=64)
+            nc.scalar.copy(out=dzg[:], in_=dz[:].rearrange("p j f -> p f j"))
+            dzg_t[c] = dzg
+            fg = stream.tile([P, PASS, J], BF16, name="fg%d" % c, tag="fg", bufs=2, align_bytes=64)
+            fg_words = fg[:].rearrange("q c t -> q (c t)").bitcast(F32)
+            for jp in range(2):
+                nc.scalar.copy(
+                    out=fg_words[:, jp * PASS:(jp + 1) * PASS].rearrange("q (l p u) -> q l p u", l=2, u=2),
+                    in_=tps[jp][:].rearrange("q l u p -> q l p u"))
+            fg_t[c] = fg
+
+        def quantize(c):
+            tcod = stream.tile([P, PASS], U32, name="tc%d" % c, tag="tcod", bufs=3, align_bytes=64)
+            tsc = stream.tile([P, PASS], U8, name="ts%d" % c, tag="tsc", bufs=3, align_bytes=64)
+            nc.vector.quantize_mx(out=tcod[:].bitcast(E5), scales=tsc[:],
+                                  in_=dzg_t[c][:].rearrange("p f j -> p (f j)"))
+            nc.vector.quantize_mx(out=fc[:, c, :].bitcast(E5), scales=fs[:, c, :],
+                                  in_=fg_t[c][:].rearrange("q c t -> q (c t)"))
+            tc_t[c] = tcod
+            ts_t[c] = tsc
+
+        def mm_dw(c):
+            h, g = divmod(c, G)
+            for m in range(4):
+                if g == 0:
+                    acc1[m] = psum.tile([P, PASS], F32, name="acc1_%d_%d" % (h, m), tag="acc1_%d" % m)
+                cols = slice(m * P, (m + 1) * P)
+                nc.tensor.matmul_mx(out=acc1[m][:], lhsT=xc[:, g, cols].bitcast(E4), lhsT_scale=xs[:, g, cols],
+                                    rhs=tc_t[c][:].bitcast(E5), rhs_scale=ts_t[c][:],
+                                    start=(g == 0), stop=(g == G - 1))
+
+        def mm_dx(g, js):
+            for j in js:
+                acc = psum.tile([P, PASS], F32, name="acc0_%d_%d" % (g, j), tag="acc0", bufs=2)
+                cols = slice(j * P, (j + 1) * P)
+                for h in range(H):
+                    nc.tensor.matmul_mx(out=acc[:], lhsT=fc[:, h * G + g, cols].bitcast(E5),
+                                        lhsT_scale=fs[:, h * G + g, cols],
+                                        rhs=wc[:, h, :].bitcast(E4), rhs_scale=ws[:, h, :],
+                                        start=(h == 0), stop=(h == H - 1))
+                acc0[(g, j)] = acc
+
+        def out_dx(g, js):
+            if js[0] == 0:
+                o0_t[g] = stream.tile([P, J, PASS], F32, name="o0_%d" % g, tag="o0", bufs=2)
+            for j in js:
+                nc.vector.scalar_tensor_tensor(out=o0_t[g][:, j, :], in0=g1_sb[g][:, j, :], scalar=wf[:, 0:1],
+                                               in1=acc0[(g, j)][:], op0=ALU.mult, op1=ALU.add)
+            nc.sync.dma_start(out=o0_v[g][:, js[0]:js[-1] + 1, :], in_=o0_t[g][:, js[0]:js[-1] + 1, :])
+
+        def out_dw(h):
+            for m in range(4):
+                o1 = stream.tile([P, PASS], F32, name="o1_%d_%d" % (h, m), tag="o1", bufs=4)
+                nc.scalar.copy(out=o1[:], in_=acc1[m][:])
+                nc.sync.dma_start(out=out_1[m * P:(m + 1) * P, h * PASS:(h + 1) * PASS], in_=o1[:])
+
+        for i in range(-1, NCH + 2):
+            if 3 <= i + 3 < NCH:
+                load_chunk(i + 3)
+            if 2 <= i < 2 + G:
+                load_g1(i - 2)
+            if 0 <= i + 1 < NCH:
+                reduce_range(i + 1)
+                sine(i + 1)
+            if G <= i - 2 < NCH:
+                out_dx(i - 2 - G, [0, 1])
+                mm_dx(i - 2 - G, [2, 3])
+            if 0 <= i < NCH:
+                make_dz(i)
+                turn(i)
+            if G <= i - 2 < NCH:
+                out_dx(i - 2 - G, [2, 3])
+            if i == 0:
+                x_interleave(3, False)
+            if i == 1:
+                x_quantize(3)
+                w_turn(0)
+            if i == 2:
+                w_quantize(0)
+                w_turn(1)
+            if i == 3:
+                w_quantize(1)
+            if 0 <= i - 1 < NCH:
+                quantize(i - 1)
+                mm_dw(i - 1)
+                if i - 1 >= G:
+                    mm_dx(i - 1 - G, [0, 1])
+                if (i - 1) % G == G - 1:
+                    out_dw((i - 1) // G)

@@ -72,10 +72,11 @@ def tile_time2vec_t_v_kernel(tc, x, W, P_vec, w, p_sc, sine_w, cosine_w, z, grad
 
         def load_chunk(c):
             h, g = divmod(c, G)
-            zt = stream.tile([P, J, PASS], F32, name="z%d" % c, tag="z", bufs=4)
-            nc.sync.dma_start(out=zt[:], in_=z_v[g][:, :, h * PASS:(h + 1) * PASS])
-            gt = stream.tile([P, J, PASS], BF16, name="g2_%d" % c, tag="g2", bufs=4)
-            nc.sync.dma_start(out=gt[:], in_=go_v[g][:, :, PASS * (1 + h):PASS * (2 + h)])
+            zt = stream.tile([P, J * PASS], F32, name="z%d" % c, tag="z", bufs=4)
+            nc.sync.dma_start(out=zt[:].rearrange("p (j f) -> p j f", j=J), in_=z_v[g][:, :, h * PASS:(h + 1) * PASS])
+            gt = stream.tile([P, J * PASS], BF16, name="g2_%d" % c, tag="g2", bufs=4)
+            nc.sync.dma_start(out=gt[:].rearrange("p (j f) -> p j f", j=J),
+                              in_=go_v[g][:, :, PASS * (1 + h):PASS * (2 + h)])
             z_sb[c] = zt
             g2_sb[c] = gt
 
@@ -84,11 +85,24 @@ def tile_time2vec_t_v_kernel(tc, x, W, P_vec, w, p_sc, sine_w, cosine_w, z, grad
             nc.sync.dma_start(out=gt[:], in_=go_v[g][:, :, 0:PASS])
             g1_sb[g] = gt
 
-        load_chunk(0)
         w_sb = keep.tile([P, 4, 2 * PASS], BF16, name="w_sb", tag="w_sb")
         nc.sync.dma_start(out=w_sb[:], in_=w_v)
+        load_chunk(0)
         load_chunk(1)
         load_chunk(2)
+
+        xc = keep.tile([P, G, PASS], U32, name="xc", tag="xc", align_bytes=64)
+        xs = keep.tile([P, G, PASS], U8, name="xs", tag="xs", align_bytes=64)
+        xg_t = {}
+
+        def x_interleave(g, lo, hi):
+            if lo == 0:
+                xg_t[g] = stream.tile([P, PASS, J], BF16, name="xg%d" % g, tag="xg", bufs=2, align_bytes=64)
+            nc.vector.tensor_copy(out=xg_t[g][:, lo:hi, :], in_=x_sb[g][:, :, lo:hi].rearrange("p j f -> p f j"))
+
+        def x_quantize(g):
+            nc.vector.quantize_mx(out=xc[:, g, :].bitcast(E4), scales=xs[:, g, :],
+                                  in_=xg_t[g][:].rearrange("p f j -> p (f j)"))
 
         sw2 = small("sw2")
         cw2 = small("cw2")
@@ -98,79 +112,74 @@ def tile_time2vec_t_v_kernel(tc, x, W, P_vec, w, p_sc, sine_w, cosine_w, z, grad
         nc.vector.tensor_tensor(out=pr[:], in0=swb[:], in1=cwb[:], op=ALU.mult)
         n2 = small("n2")
         df = small("df")
-        nc.vector.tensor_tensor(out=n2[:], in0=sw2[:], in1=cw2[:], op=ALU.add)
+        nc.vector.scalar_tensor_tensor(out=n2[:], in0=sw2[:], scalar=1e-30, in1=cw2[:], op0=ALU.add, op1=ALU.add)
         nc.vector.tensor_tensor(out=df[:], in0=cw2[:], in1=sw2[:], op=ALU.subtract)
-        n2c = small("n2c")
-        nc.vector.tensor_scalar_max(out=n2c[:], in0=n2[:], scalar1=1e-30)
-        two_or_0 = small("two_or_0")
-        nc.vector.tensor_scalar(out=two_or_0[:], in0=df[:], scalar1=0.0, scalar2=2.0, op0=ALU.is_ge, op1=ALU.mult)
         inv = small("inv")
-        nc.vector.reciprocal(out=inv[:], in_=n2c[:])
-        q = small("q")
-        nc.vector.tensor_scalar(out=q[:], in0=two_or_0[:], scalar1=1.0, scalar2=inv[:, 0:1],
-                                op0=ALU.subtract, op1=ALU.mult)
-        s2 = small("s2")
-        nc.vector.tensor_scalar(out=s2[:], in0=pr[:], scalar1=q[:, 0:1], scalar2=-2.0, op0=ALU.mult, op1=ALU.mult)
-        nc2 = small("nc2")
-        nc.vector.tensor_scalar(out=nc2[:], in0=df[:], scalar1=q[:, 0:1], scalar2=-1.0, op0=ALU.mult, op1=ALU.mult)
-        pair = small("pair", 2)
-        nc.vector.tensor_copy(out=pair[:, 0:1], in_=s2[:])
-        nc.vector.tensor_scalar_add(out=pair[:, 1:2], in0=s2[:], scalar1=0.5 * PI)
+        nc.vector.reciprocal(out=inv[:], in_=n2[:])
+        t4 = small("t4")
+        nc.vector.tensor_scalar(out=t4[:], in0=df[:], scalar1=0.0, scalar2=-4.0, op0=ALU.is_ge, op1=ALU.mult)
+        x_interleave(0, 0, 256)
+        q2 = small("q2")
+        nc.vector.tensor_scalar(out=q2[:], in0=t4[:], scalar1=2.0, scalar2=inv[:, 0:1], op0=ALU.add, op1=ALU.mult)
         off = small("off")
-        nc.vector.tensor_scalar(out=off[:], in0=two_or_0[:], scalar1=-0.25 * PI, scalar2=0.5 * PI,
+        nc.vector.tensor_scalar(out=off[:], in0=t4[:], scalar1=0.125 * PI, scalar2=0.5 * PI, op0=ALU.mult, op1=ALU.add)
+        x_interleave(0, 256, PASS)
+        pair = small("pair", 2)
+        nc.vector.tensor_scalar_mul(out=pair[:, 0:1], in0=pr[:], scalar1=q2[:, 0:1])
+        nc.vector.tensor_scalar(out=pair[:, 1:2], in0=pr[:], scalar1=q2[:, 0:1], scalar2=0.5 * PI,
                                 op0=ALU.mult, op1=ALU.add)
+        nc2 = small("nc2")
+        nc.vector.tensor_scalar(out=nc2[:], in0=df[:], scalar1=q2[:, 0:1], scalar2=0.5, op0=ALU.mult, op1=ALU.mult)
+        s2 = pair[:, 0:1]
+
+        moved = None
+        for it in range(3):
+            sc = small("sc%d" % it, 2)
+            part = small("part%d" % it)
+            nxt = small("moved%d" % it)
+            if moved is None:
+                nc.scalar.activation(out=sc[:], in_=pair[:], func=ACT.Sin)
+                nc.scalar.activation(out=part[:], in_=sc[:, 1:2], func=ACT.Copy, scale=s2)
+            else:
+                nc.scalar.activation(out=sc[:], in_=pair[:], func=ACT.Sin, scale=1.0, bias=moved[:, 0:1])
+                nc.scalar.activation(out=part[:], in_=sc[:, 1:2], func=ACT.Identity, scale=s2, bias=moved[:, 0:1])
+            nc.scalar.activation(out=nxt[:], in_=sc[:, 0:1], func=ACT.Identity, scale=nc2[:, 0:1], bias=part[:, 0:1])
+            moved = nxt
+
+        x_interleave(1, 0, 256)
+        offp = small("offp")
+        nc.vector.tensor_scalar(out=offp[:], in0=s2, scalar1=0.5, scalar2=off[:, 0:1], op0=ALU.mult, op1=ALU.add)
+        x_interleave(1, 256, PASS)
+        offt = small("offt")
+        nc.vector.tensor_scalar_mul(out=offt[:], in0=offp[:], scalar1=1.0 / TWO_PI)
+        hp = small("hp")
+        nc.vector.tensor_scalar(out=hp[:], in0=offp[:], scalar1=-1.0, scalar2=0.5 * PI, op0=ALU.mult, op1=ALU.add)
         swf = small("swf")
         ncw = small("ncw")
-        wf = small("wf")
         nc.vector.tensor_copy(out=swf[:], in_=swb[:])
         nc.vector.tensor_scalar_mul(out=ncw[:], in0=cwb[:], scalar1=-1.0)
 
-        sc = small("sc", 2)
-        mm = small("mm")
-        dd = small("dd")
-        for it in range(3):
-            nc.scalar.activation(out=sc[:], in_=pair[:], func=ACT.Sin)
-            nc.scalar.activation(out=mm[:], in_=sc[:, 1:2], func=ACT.Copy, scale=s2[:, 0:1])
-            nc.scalar.activation(out=dd[:], in_=sc[:, 0:1], func=ACT.Identity, scale=nc2[:, 0:1], bias=mm[:, 0:1])
-            nc.scalar.activation(out=pair[:], in_=pair[:], func=ACT.Identity, scale=1.0, bias=dd[:, 0:1])
-        phi = small("phi")
-        nc.scalar.activation(out=phi[:], in_=pair[:, 0:1], func=ACT.Identity, scale=0.5, bias=off[:, 0:1])
         turns = small("turns")
-        nc.scalar.activation(out=turns[:], in_=phi[:], func=ACT.Copy, scale=1.0 / TWO_PI)
-
-        xc = keep.tile([P, G, PASS], U32, name="xc", tag="xc", align_bytes=64)
-        xs = keep.tile([P, G, PASS], U8, name="xs", tag="xs", align_bytes=64)
-        xg_t = {}
-
-        def x_interleave(g, on_vector):
-            xg = stream.tile([P, PASS, J], BF16, name="xg%d" % g, tag="xg", bufs=2, align_bytes=64)
-            if on_vector:
-                nc.vector.tensor_copy(out=xg[:], in_=x_sb[g][:].rearrange("p j f -> p f j"))
-            else:
-                nc.scalar.copy(out=xg[:], in_=x_sb[g][:].rearrange("p j f -> p f j"))
-            xg_t[g] = xg
-
-        def x_quantize(g):
-            nc.vector.quantize_mx(out=xc[:, g, :].bitcast(E4), scales=xs[:, g, :],
-                                  in_=xg_t[g][:].rearrange("p f j -> p (f j)"))
-
-        x_interleave(0, True)
-        x_interleave(1, True)
-        x_quantize(0)
-        x_interleave(2, True)
-        x_quantize(1)
-        nc.vector.tensor_copy(out=wf[:], in_=wb[:])
-        x_quantize(2)
-
-        pa = small("pa", 2)
-        nc.vector.tensor_copy(out=pa[:, 0:1], in_=phi[:])
-        nc.vector.tensor_scalar(out=pa[:, 1:2], in0=phi[:], scalar1=-1.0, scalar2=0.5 * PI, op0=ALU.mult, op1=ALU.add)
-        sc2 = small("sc2", 2)
-        nc.scalar.activation(out=sc2[:], in_=pa[:], func=ACT.Sin)
+        nc.scalar.activation(out=turns[:], in_=moved[:], func=ACT.Identity, scale=0.5 / TWO_PI, bias=offt[:, 0:1])
+        phi = small("phi")
+        nc.scalar.activation(out=phi[:], in_=moved[:], func=ACT.Identity, scale=0.5, bias=offp[:, 0:1])
+        sin_phi = small("sin_phi")
+        nc.scalar.activation(out=sin_phi[:], in_=phi[:], func=ACT.Sin)
+        cos_phi = small("cos_phi")
+        nc.scalar.activation(out=cos_phi[:], in_=moved[:], func=ACT.Sin, scale=-0.5, bias=hp[:, 0:1])
         m2 = small("m2")
-        nc.scalar.activation(out=m2[:], in_=sc2[:, 0:1], func=ACT.Copy, scale=swf[:, 0:1])
+        nc.scalar.activation(out=m2[:], in_=sin_phi[:], func=ACT.Copy, scale=swf[:, 0:1])
         amp = small("amp")
-        nc.scalar.activation(out=amp[:], in_=sc2[:, 1:2], func=ACT.Identity, scale=ncw[:, 0:1], bias=m2[:, 0:1])
+        nc.scalar.activation(out=amp[:], in_=cos_phi[:], func=ACT.Identity, scale=ncw[:, 0:1], bias=m2[:, 0:1])
+
+        x_quantize(0)
+        x_interleave(2, 0, PASS)
+        x_quantize(1)
+        x_interleave(3, 0, PASS)
+        x_quantize(2)
+        wf = small("wf")
+        nc.vector.tensor_copy(out=wf[:], in_=wb[:])
+        x_quantize(3)
 
         wc = keep.tile([P, H, PASS], U32, name="wc", tag="wc", align_bytes=64)
         ws = keep.tile([P, H, PASS], U8, name="ws", tag="ws", align_bytes=64)
@@ -195,49 +204,46 @@ def tile_time2vec_t_v_kernel(tc, x, W, P_vec, w, p_sc, sine_w, cosine_w, z, grad
             nc.vector.quantize_mx(out=wc[:, h, :].bitcast(E4), scales=ws[:, h, :],
                                   in_=wg_t[h][:].rearrange("q c t -> q (c t)"))
 
+        w_turn(0)
+        w_turn(1)
+
         fc = keep.tile([P, NCH, PASS], U32, name="fc", tag="fc", align_bytes=64)
         fs = keep.tile([P, NCH, PASS], U8, name="fs", tag="fs", align_bytes=64)
+        k_t = {}
         dz_t = {}
         dzg_t = {}
         fg_t = {}
+        tp_t = {}
         tc_t = {}
         ts_t = {}
         acc1 = {}
         acc0 = {}
-        o0_t = {}
 
-        def reduce_range(c):
-            zf = z_sb[c][:].rearrange("p j f -> p (j f)")
-            kt = stream.tile([P, J * PASS], I32, name="k%d" % c, tag="k", bufs=2)
-            for a in range(2):
-                cols = slice(a * HALF, (a + 1) * HALF)
-                nc.vector.tensor_scalar(out=kt[:, cols], in0=zf[:, cols], scalar1=1.0 / TWO_PI,
-                                        scalar2=turns[:, 0:1], op0=ALU.mult, op1=ALU.add)
-            for a in range(2):
-                cols = slice(a * HALF, (a + 1) * HALF)
-                nc.vector.scalar_tensor_tensor(out=zf[:, cols], in0=kt[:, cols], scalar=-TWO_PI, in1=zf[:, cols],
-                                               op0=ALU.mult, op1=ALU.add)
+        def reduce_k(c, a):
+            if a == 0:
+                k_t[c] = stream.tile([P, J * PASS], I32, name="k%d" % c, tag="k", bufs=2)
+            cols = slice(a * HALF, (a + 1) * HALF)
+            nc.vector.tensor_scalar(out=k_t[c][:, cols], in0=z_sb[c][:, cols], scalar1=1.0 / TWO_PI,
+                                    scalar2=turns[:, 0:1], op0=ALU.mult, op1=ALU.add)
 
-        def sine(c):
-            zf = z_sb[c][:].rearrange("p j f -> p (j f)")
-            for a in range(2):
-                cols = slice(a * HALF, (a + 1) * HALF)
-                nc.scalar.activation(out=zf[:, cols], in_=zf[:, cols], func=ACT.Sin, bias=phi[:, 0:1], scale=1.0)
+        def reduce_r(c, a):
+            cols = slice(a * HALF, (a + 1) * HALF)
+            nc.vector.scalar_tensor_tensor(out=z_sb[c][:, cols], in0=k_t[c][:, cols], scalar=-TWO_PI,
+                                           in1=z_sb[c][:, cols], op0=ALU.mult, op1=ALU.add)
 
-        def make_dz(c):
-            zf = z_sb[c][:].rearrange("p j f -> p (j f)")
-            gf = g2_sb[c][:].rearrange("p j f -> p (j f)")
-            dz = stream.tile([P, J, PASS], BF16, name="dz%d" % c, tag="dz", bufs=3)
-            dzf = dz[:].rearrange("p j f -> p (j f)")
-            for a in range(2):
-                cols = slice(a * HALF, (a + 1) * HALF)
-                nc.vector.scalar_tensor_tensor(out=dzf[:, cols], in0=zf[:, cols], scalar=amp[:, 0:1],
-                                               in1=gf[:, cols], op0=ALU.mult, op1=ALU.mult)
-            dz_t[c] = dz
+        def sine(c, a):
+            cols = slice(a * HALF, (a + 1) * HALF)
+            nc.scalar.activation(out=z_sb[c][:, cols], in_=z_sb[c][:, cols], func=ACT.Sin, bias=phi[:, 0:1], scale=1.0)
+
+        def make_dz(c, a):
+            if a == 0:
+                dz_t[c] = stream.tile([P, J * PASS], BF16, name="dz%d" % c, tag="dz", bufs=3)
+            cols = slice(a * HALF, (a + 1) * HALF)
+            nc.vector.scalar_tensor_tensor(out=dz_t[c][:, cols], in0=z_sb[c][:, cols], scalar=amp[:, 0:1],
+                                           in1=g2_sb[c][:, cols], op0=ALU.mult, op1=ALU.mult)
 
         def turn(c):
-            dz = dz_t[c]
-            words = dz[:].rearrange("p j f -> p (j f)").bitcast(F32)
+            words = dz_t[c][:].bitcast(F32)
             tps = []
             for jp in range(2):
                 tp = psum.tile([P, 2, 2, P], F32, name="tp%d_%d" % (c, jp), tag="tp", bufs=2)
@@ -246,92 +252,150 @@ def tile_time2vec_t_v_kernel(tc, x, W, P_vec, w, p_sc, sine_w, cosine_w, z, grad
                     for u in range(2):
                         nc.tensor.transpose(tp[:, l, u, :], words[:, base + u:base + 256:2], ident[:])
                 tps.append(tp)
+            tp_t[c] = tps
+
+        def interleave(c):
             dzg = stream.tile([P, PASS, J], BF16, name="dzg%d" % c, tag="dzg", bufs=2, align_bytes=64)
-            nc.scalar.copy(out=dzg[:], in_=dz[:].rearrange("p j f -> p f j"))
+            nc.scalar.copy(out=dzg[:], in_=dz_t[c][:].rearrange("p (j f) -> p f j", j=J))
             dzg_t[c] = dzg
+
+        def gather(c):
             fg = stream.tile([P, PASS, J], BF16, name="fg%d" % c, tag="fg", bufs=2, align_bytes=64)
             fg_words = fg[:].rearrange("q c t -> q (c t)").bitcast(F32)
             for jp in range(2):
                 nc.scalar.copy(
                     out=fg_words[:, jp * PASS:(jp + 1) * PASS].rearrange("q (l p u) -> q l p u", l=2, u=2),
-                    in_=tps[jp][:].rearrange("q l u p -> q l p u"))
+                    in_=tp_t[c][jp][:].rearrange("q l u p -> q l p u"))
             fg_t[c] = fg
 
-        def quantize(c):
+        def quantize_f(c):
+            nc.vector.quantize_mx(out=fc[:, c, :].bitcast(E5), scales=fs[:, c, :],
+                                  in_=fg_t[c][:].rearrange("q c t -> q (c t)"))
+
+        def quantize_t(c):
             tcod = stream.tile([P, PASS], U32, name="tc%d" % c, tag="tcod", bufs=3, align_bytes=64)
             tsc = stream.tile([P, PASS], U8, name="ts%d" % c, tag="tsc", bufs=3, align_bytes=64)
             nc.vector.quantize_mx(out=tcod[:].bitcast(E5), scales=tsc[:],
                                   in_=dzg_t[c][:].rearrange("p f j -> p (f j)"))
-            nc.vector.quantize_mx(out=fc[:, c, :].bitcast(E5), scales=fs[:, c, :],
-                                  in_=fg_t[c][:].rearrange("q c t -> q (c t)"))
             tc_t[c] = tcod
             ts_t[c] = tsc
 
-        def mm_dw(c):
+        def mm_dw(c, m):
             h, g = divmod(c, G)
-            for m in range(4):
-                if g == 0:
-                    acc1[m] = psum.tile([P, PASS], F32, name="acc1_%d_%d" % (h, m), tag="acc1_%d" % m)
-                cols = slice(m * P, (m + 1) * P)
-                nc.tensor.matmul_mx(out=acc1[m][:], lhsT=xc[:, g, cols].bitcast(E4), lhsT_scale=xs[:, g, cols],
-                                    rhs=tc_t[c][:].bitcast(E5), rhs_scale=ts_t[c][:],
-                                    start=(g == 0), stop=(g == G - 1))
+            if g == 0:
+                acc1[m] = psum.tile([P, PASS], F32, name="acc1_%d_%d" % (h, m), tag="acc1_%d" % m)
+            cols = slice(m * P, (m + 1) * P)
+            nc.tensor.matmul_mx(out=acc1[m][:], lhsT=xc[:, g, cols].bitcast(E4), lhsT_scale=xs[:, g, cols],
+                                rhs=tc_t[c][:].bitcast(E5), rhs_scale=ts_t[c][:],
+                                start=(g == 0), stop=(g == G - 1))
 
-        def mm_dx(g, js):
-            for j in js:
-                acc = psum.tile([P, PASS], F32, name="acc0_%d_%d" % (g, j), tag="acc0", bufs=2)
-                cols = slice(j * P, (j + 1) * P)
-                for h in range(H):
-                    nc.tensor.matmul_mx(out=acc[:], lhsT=fc[:, h * G + g, cols].bitcast(E5),
-                                        lhsT_scale=fs[:, h * G + g, cols],
-                                        rhs=wc[:, h, :].bitcast(E4), rhs_scale=ws[:, h, :],
-                                        start=(h == 0), stop=(h == H - 1))
-                acc0[(g, j)] = acc
+        def mm_dx(g, j, tag):
+            acc = psum.tile([P, PASS], F32, name="acc0_%d_%d" % (g, j), tag=tag, bufs=2)
+            cols = slice(j * P, (j + 1) * P)
+            for h in range(H):
+                nc.tensor.matmul_mx(out=acc[:], lhsT=fc[:, h * G + g, cols].bitcast(E5),
+                                    lhsT_scale=fs[:, h * G + g, cols],
+                                    rhs=wc[:, h, :].bitcast(E4), rhs_scale=ws[:, h, :],
+                                    start=(h == 0), stop=(h == H - 1))
+            acc0[(g, j)] = acc
 
-        def out_dx(g, js):
-            if js[0] == 0:
-                o0_t[g] = stream.tile([P, J, PASS], F32, name="o0_%d" % g, tag="o0", bufs=2)
-            for j in js:
-                nc.vector.scalar_tensor_tensor(out=o0_t[g][:, j, :], in0=g1_sb[g][:, j, :], scalar=wf[:, 0:1],
-                                               in1=acc0[(g, j)][:], op0=ALU.mult, op1=ALU.add)
-            nc.sync.dma_start(out=o0_v[g][:, js[0]:js[-1] + 1, :], in_=o0_t[g][:, js[0]:js[-1] + 1, :])
+        def out_dx(g, j):
+            o0 = stream.tile([P, PASS], F32, name="o0_%d_%d" % (g, j), tag="o0", bufs=8)
+            nc.vector.scalar_tensor_tensor(out=o0[:], in0=g1_sb[g][:, j, :], scalar=wf[:, 0:1],
+                                           in1=acc0[(g, j)][:], op0=ALU.mult, op1=ALU.add)
+            nc.sync.dma_start(out=o0_v[g][:, j, :], in_=o0[:])
 
         def out_dw(h):
             for m in range(4):
                 o1 = stream.tile([P, PASS], F32, name="o1_%d_%d" % (h, m), tag="o1", bufs=4)
                 nc.scalar.copy(out=o1[:], in_=acc1[m][:])
-                nc.sync.dma_start(out=out_1[m * P:(m + 1) * P, h * PASS:(h + 1) * PASS], in_=o1[:])
+                nc.scalar.dma_start(out=out_1[m * P:(m + 1) * P, h * PASS:(h + 1) * PASS], in_=o1[:])
+
+        LAST = NCH - 1
+
+        def step(i):
+            has_n = 0 <= i + 1 < NCH
+            has_c = 0 <= i < NCH
+            has_q = 0 <= i - 1 < NCH
+            has_w = 0 <= i - 2 < LAST
+            has_o = G <= i - 2 < NCH
+            starts_dx = has_q and i - 1 >= G
+            go = i - 2 - G
+            if has_o:
+                out_dx(go, 0)
+                if go < G - 1:
+                    mm_dx(go, 2, "acc0")
+            if has_w:
+                mm_dw(i - 2, 0)
+            if has_c:
+                make_dz(i, 0)
+            if has_n:
+                reduce_k(i + 1, 0)
+            if has_o:
+                out_dx(go, 1)
+                if go < G - 1:
+                    mm_dx(go, 3, "acc0")
+            if has_w:
+                mm_dw(i - 2, 1)
+            if has_c:
+                make_dz(i, 1)
+                interleave(i)
+                turn(i)
+            if has_q:
+                quantize_f(i - 1)
+            if has_o:
+                out_dx(go, 2)
+            if starts_dx:
+                mm_dx(i - 1 - G, 0, "acc0")
+            if has_w:
+                mm_dw(i - 2, 2)
+            if has_n:
+                reduce_k(i + 1, 1)
+                reduce_r(i + 1, 0)
+                sine(i + 1, 0)
+            if has_o:
+                out_dx(go, 3)
+            if starts_dx:
+                mm_dx(i - 1 - G, 1, "acc0")
+            if has_w:
+                mm_dw(i - 2, 3)
+            if has_q:
+                quantize_t(i - 1)
+            if has_n:
+                reduce_r(i + 1, 1)
+                sine(i + 1, 1)
+            if has_c:
+                gather(i)
+            if has_w and (i - 2) % G == G - 1:
+                out_dw((i - 2) // G)
+            if i == 0 or i == 1:
+                w_quantize(i)
+
+        def last_but_one_step():
+            out_dx(G - 2, 0)
+            mm_dx(G - 2, 2, "acc0")
+            for m in range(4):
+                mm_dw(LAST - 1, m)
+            out_dx(G - 2, 1)
+            mm_dx(G - 2, 3, "acc0")
+            quantize_t(LAST)
+            for m in range(4):
+                mm_dw(LAST, m)
+            out_dw(H - 1)
+            quantize_f(LAST)
+            mm_dx(G - 1, 0, "tp")
+            mm_dx(G - 1, 1, "tp")
+            out_dx(G - 2, 2)
+            mm_dx(G - 1, 2, "acc0")
+            out_dx(G - 2, 3)
+            mm_dx(G - 1, 3, "acc0")
 
         for i in range(-1, NCH + 2):
             if 3 <= i + 3 < NCH:
                 load_chunk(i + 3)
             if 2 <= i < 2 + G:
                 load_g1(i - 2)
-            if 0 <= i + 1 < NCH:
-                reduce_range(i + 1)
-                sine(i + 1)
-            if G <= i - 2 < NCH:
-                out_dx(i - 2 - G, [0, 1])
-                mm_dx(i - 2 - G, [2, 3])
-            if 0 <= i < NCH:
-                make_dz(i)
-                turn(i)
-            if G <= i - 2 < NCH:
-                out_dx(i - 2 - G, [2, 3])
-            if i == 0:
-                x_interleave(3, False)
-            if i == 1:
-                x_quantize(3)
-                w_turn(0)
-            if i == 2:
-                w_quantize(0)
-                w_turn(1)
-            if i == 3:
-                w_quantize(1)
-            if 0 <= i - 1 < NCH:
-                quantize(i - 1)
-                mm_dw(i - 1)
-                if i - 1 >= G:
-                    mm_dx(i - 1 - G, [0, 1])
-                if (i - 1) % G == G - 1:
-                    out_dw((i - 1) // G)
+            if i == NCH:
+                last_but_one_step()
+            else:
+                step(i)

@@ -60,11 +60,12 @@ def tile_time2vec_t_v_kernel(tc, x, W, P_vec, w, p_sc, sine_w, cosine_w, z, grad
         ident = const.tile([P, P], F32, name="ident", tag="ident")
         make_identity(nc, ident[:])
 
-        x_sb = []
-        for g in range(G):
+        x_sb = {}
+
+        def load_x(g):
             xt = keep.tile([P, J, PASS], BF16, name="x%d" % g, tag="x%d" % g)
             nc.sync.dma_start(out=xt[:], in_=x_v[g])
-            x_sb.append(xt)
+            x_sb[g] = xt
 
         z_sb = {}
         g2_sb = {}
@@ -85,9 +86,13 @@ def tile_time2vec_t_v_kernel(tc, x, W, P_vec, w, p_sc, sine_w, cosine_w, z, grad
             nc.sync.dma_start(out=gt[:], in_=go_v[g][:, :, 0:PASS])
             g1_sb[g] = gt
 
+        load_x(0)
+        load_x(1)
+        load_x(2)
+        load_chunk(0)
+        load_x(3)
         w_sb = keep.tile([P, 4, 2 * PASS], BF16, name="w_sb", tag="w_sb")
         nc.sync.dma_start(out=w_sb[:], in_=w_v)
-        load_chunk(0)
         load_chunk(1)
         load_chunk(2)
 
@@ -95,91 +100,78 @@ def tile_time2vec_t_v_kernel(tc, x, W, P_vec, w, p_sc, sine_w, cosine_w, z, grad
         xs = keep.tile([P, G, PASS], U8, name="xs", tag="xs", align_bytes=64)
         xg_t = {}
 
-        def x_interleave(g, lo, hi):
-            if lo == 0:
-                xg_t[g] = stream.tile([P, PASS, J], BF16, name="xg%d" % g, tag="xg", bufs=2, align_bytes=64)
-            nc.vector.tensor_copy(out=xg_t[g][:, lo:hi, :], in_=x_sb[g][:, :, lo:hi].rearrange("p j f -> p f j"))
+        def x_interleave(g, engine_copy):
+            xg_t[g] = stream.tile([P, PASS, J], BF16, name="xg%d" % g, tag="xg", bufs=2, align_bytes=64)
+            engine_copy(out=xg_t[g][:], in_=x_sb[g][:].rearrange("p j f -> p f j"))
 
         def x_quantize(g):
             nc.vector.quantize_mx(out=xc[:, g, :].bitcast(E4), scales=xs[:, g, :],
                                   in_=xg_t[g][:].rearrange("p f j -> p (f j)"))
 
-        sw2 = small("sw2")
-        cw2 = small("cw2")
-        pr = small("pr")
-        nc.vector.tensor_tensor(out=sw2[:], in0=swb[:], in1=swb[:], op=ALU.mult)
-        nc.vector.tensor_tensor(out=cw2[:], in0=cwb[:], in1=cwb[:], op=ALU.mult)
-        nc.vector.tensor_tensor(out=pr[:], in0=swb[:], in1=cwb[:], op=ALU.mult)
-        n2 = small("n2")
-        df = small("df")
-        nc.vector.scalar_tensor_tensor(out=n2[:], in0=sw2[:], scalar=1e-30, in1=cw2[:], op0=ALU.add, op1=ALU.add)
-        nc.vector.tensor_tensor(out=df[:], in0=cw2[:], in1=sw2[:], op=ALU.subtract)
-        inv = small("inv")
-        nc.vector.reciprocal(out=inv[:], in_=n2[:])
-        t4 = small("t4")
-        nc.vector.tensor_scalar(out=t4[:], in0=df[:], scalar1=0.0, scalar2=-4.0, op0=ALU.is_ge, op1=ALU.mult)
-        x_interleave(0, 0, 256)
-        q2 = small("q2")
-        nc.vector.tensor_scalar(out=q2[:], in0=t4[:], scalar1=2.0, scalar2=inv[:, 0:1], op0=ALU.add, op1=ALU.mult)
-        off = small("off")
-        nc.vector.tensor_scalar(out=off[:], in0=t4[:], scalar1=0.125 * PI, scalar2=0.5 * PI, op0=ALU.mult, op1=ALU.add)
-        x_interleave(0, 256, PASS)
-        pair = small("pair", 2)
-        nc.vector.tensor_scalar_mul(out=pair[:, 0:1], in0=pr[:], scalar1=q2[:, 0:1])
-        nc.vector.tensor_scalar(out=pair[:, 1:2], in0=pr[:], scalar1=q2[:, 0:1], scalar2=0.5 * PI,
-                                op0=ALU.mult, op1=ALU.add)
-        nc2 = small("nc2")
-        nc.vector.tensor_scalar(out=nc2[:], in0=df[:], scalar1=q2[:, 0:1], scalar2=0.5, op0=ALU.mult, op1=ALU.mult)
-        s2 = pair[:, 0:1]
-
-        moved = None
-        for it in range(3):
-            sc = small("sc%d" % it, 2)
-            part = small("part%d" % it)
-            nxt = small("moved%d" % it)
-            if moved is None:
-                nc.scalar.activation(out=sc[:], in_=pair[:], func=ACT.Sin)
-                nc.scalar.activation(out=part[:], in_=sc[:, 1:2], func=ACT.Copy, scale=s2)
+        def fma(name, in_, scale, bias=None, cols=None):
+            out = cols if cols is not None else small(name)[:]
+            if bias is None:
+                nc.scalar.activation(out=out, in_=in_, func=ACT.Copy, scale=scale)
             else:
-                nc.scalar.activation(out=sc[:], in_=pair[:], func=ACT.Sin, scale=1.0, bias=moved[:, 0:1])
-                nc.scalar.activation(out=part[:], in_=sc[:, 1:2], func=ACT.Identity, scale=s2, bias=moved[:, 0:1])
-            nc.scalar.activation(out=nxt[:], in_=sc[:, 0:1], func=ACT.Identity, scale=nc2[:, 0:1], bias=part[:, 0:1])
-            moved = nxt
+                nc.scalar.activation(out=out, in_=in_, func=ACT.Identity, scale=scale, bias=bias)
+            return out
 
-        x_interleave(1, 0, 256)
-        offp = small("offp")
-        nc.vector.tensor_scalar(out=offp[:], in0=s2, scalar1=0.5, scalar2=off[:, 0:1], op0=ALU.mult, op1=ALU.add)
-        x_interleave(1, 256, PASS)
-        offt = small("offt")
-        nc.vector.tensor_scalar_mul(out=offt[:], in0=offp[:], scalar1=1.0 / TWO_PI)
-        hp = small("hp")
-        nc.vector.tensor_scalar(out=hp[:], in0=offp[:], scalar1=-1.0, scalar2=0.5 * PI, op0=ALU.mult, op1=ALU.add)
-        swf = small("swf")
-        ncw = small("ncw")
-        nc.vector.tensor_copy(out=swf[:], in_=swb[:])
-        nc.vector.tensor_scalar_mul(out=ncw[:], in0=cwb[:], scalar1=-1.0)
+        halfpi = small("halfpi")
+        nc.vector.tensor_scalar(out=halfpi[:], in0=warm[:], scalar1=0.0, scalar2=0.5 * PI, op0=ALU.mult, op1=ALU.add)
+        sw_f = fma("sw_f", swb[:], 1.0)
+        sw_2f = fma("sw_2f", swb[:], 2.0)
+        cw_f = fma("cw_f", cwb[:], 1.0)
+        sw2 = fma("sw2", sw_f, sw_f)
+        cw2 = fma("cw2", cw_f, cw_f)
+        n2 = fma("n2", sw2, 1.0, cw2)
+        df = fma("df", sw2, -1.0, cw2)
+        pr2 = fma("pr2", sw_2f, cw_f)
+        ncw = fma("ncw", cwb[:], -1.0)
 
-        turns = small("turns")
-        nc.scalar.activation(out=turns[:], in_=moved[:], func=ACT.Identity, scale=0.5 / TWO_PI, bias=offt[:, 0:1])
-        phi = small("phi")
-        nc.scalar.activation(out=phi[:], in_=moved[:], func=ACT.Identity, scale=0.5, bias=offp[:, 0:1])
+        x_interleave(0, nc.vector.tensor_copy)
+        n2c = small("n2c")
+        nc.vector.tensor_scalar_max(out=n2c[:], in0=n2, scalar1=1e-30)
+        t2 = small("t2")
+        nc.vector.tensor_scalar(out=t2[:], in0=df, scalar1=0.0, scalar2=-2.0, op0=ALU.is_ge, op1=ALU.mult)
+        inv = small("inv")
+        nc.vector.reciprocal(out=inv[:], in_=n2c[:])
+        x_interleave(1, nc.vector.tensor_copy)
+
+        q1 = fma("q1", t2[:], inv[:], inv[:])
+        pair = small("pair", 2)
+        s2 = fma("", pr2, q1, None, pair[:, 0:1])
+        fma("", pr2, q1, halfpi[:], pair[:, 1:2])
+        nc2 = fma("nc2", df, q1)
+
+        sc0 = small("sc0", 2)
+        nc.scalar.activation(out=sc0[:], in_=pair[:], func=ACT.Sin)
+        off = fma("off", t2[:], 0.25 * PI, halfpi[:])
+        part0 = fma("part0", sc0[:, 1:2], s2)
+        offp = fma("offp", s2, 0.5, off)
+        moved = fma("moved0", sc0[:, 0:1], nc2, part0)
+        offt = fma("offt", offp, 1.0 / TWO_PI)
+        hp = fma("hp", offp, -1.0, halfpi[:])
+        for it in (1, 2):
+            sc = small("sc%d" % it, 2)
+            nc.scalar.activation(out=sc[:], in_=pair[:], func=ACT.Sin, scale=1.0, bias=moved)
+            part = fma("part%d" % it, sc[:, 1:2], s2, moved)
+            moved = fma("moved%d" % it, sc[:, 0:1], nc2, part)
+        turns = fma("turns", moved, 0.5 / TWO_PI, offt)
+        phi = fma("phi", moved, 0.5, offp)
         sin_phi = small("sin_phi")
-        nc.scalar.activation(out=sin_phi[:], in_=phi[:], func=ACT.Sin)
+        nc.scalar.activation(out=sin_phi[:], in_=phi, func=ACT.Sin)
         cos_phi = small("cos_phi")
-        nc.scalar.activation(out=cos_phi[:], in_=moved[:], func=ACT.Sin, scale=-0.5, bias=hp[:, 0:1])
-        m2 = small("m2")
-        nc.scalar.activation(out=m2[:], in_=sin_phi[:], func=ACT.Copy, scale=swf[:, 0:1])
-        amp = small("amp")
-        nc.scalar.activation(out=amp[:], in_=cos_phi[:], func=ACT.Identity, scale=ncw[:, 0:1], bias=m2[:, 0:1])
+        nc.scalar.activation(out=cos_phi[:], in_=moved, func=ACT.Sin, scale=-0.5, bias=hp)
+        m2 = fma("m2", sin_phi[:], sw_f)
+        amp = fma("amp", cos_phi[:], ncw, m2)
 
         x_quantize(0)
-        x_interleave(2, 0, PASS)
+        x_interleave(2, nc.vector.tensor_copy)
         x_quantize(1)
-        x_interleave(3, 0, PASS)
-        x_quantize(2)
         wf = small("wf")
         nc.vector.tensor_copy(out=wf[:], in_=wb[:])
-        x_quantize(3)
+        x_quantize(2)
+        x_interleave(3, nc.scalar.copy)
 
         wc = keep.tile([P, H, PASS], U32, name="wc", tag="wc", align_bytes=64)
         ws = keep.tile([P, H, PASS], U8, name="ws", tag="ws", align_bytes=64)
@@ -204,9 +196,6 @@ def tile_time2vec_t_v_kernel(tc, x, W, P_vec, w, p_sc, sine_w, cosine_w, z, grad
             nc.vector.quantize_mx(out=wc[:, h, :].bitcast(E4), scales=ws[:, h, :],
                                   in_=wg_t[h][:].rearrange("q c t -> q (c t)"))
 
-        w_turn(0)
-        w_turn(1)
-
         fc = keep.tile([P, NCH, PASS], U32, name="fc", tag="fc", align_bytes=64)
         fs = keep.tile([P, NCH, PASS], U8, name="fs", tag="fs", align_bytes=64)
         k_t = {}
@@ -224,7 +213,7 @@ def tile_time2vec_t_v_kernel(tc, x, W, P_vec, w, p_sc, sine_w, cosine_w, z, grad
                 k_t[c] = stream.tile([P, J * PASS], I32, name="k%d" % c, tag="k", bufs=2)
             cols = slice(a * HALF, (a + 1) * HALF)
             nc.vector.tensor_scalar(out=k_t[c][:, cols], in0=z_sb[c][:, cols], scalar1=1.0 / TWO_PI,
-                                    scalar2=turns[:, 0:1], op0=ALU.mult, op1=ALU.add)
+                                    scalar2=turns, op0=ALU.mult, op1=ALU.add)
 
         def reduce_r(c, a):
             cols = slice(a * HALF, (a + 1) * HALF)
@@ -233,13 +222,13 @@ def tile_time2vec_t_v_kernel(tc, x, W, P_vec, w, p_sc, sine_w, cosine_w, z, grad
 
         def sine(c, a):
             cols = slice(a * HALF, (a + 1) * HALF)
-            nc.scalar.activation(out=z_sb[c][:, cols], in_=z_sb[c][:, cols], func=ACT.Sin, bias=phi[:, 0:1], scale=1.0)
+            nc.scalar.activation(out=z_sb[c][:, cols], in_=z_sb[c][:, cols], func=ACT.Sin, bias=phi, scale=1.0)
 
         def make_dz(c, a):
             if a == 0:
                 dz_t[c] = stream.tile([P, J * PASS], BF16, name="dz%d" % c, tag="dz", bufs=3)
             cols = slice(a * HALF, (a + 1) * HALF)
-            nc.vector.scalar_tensor_tensor(out=dz_t[c][:, cols], in0=z_sb[c][:, cols], scalar=amp[:, 0:1],
+            nc.vector.scalar_tensor_tensor(out=dz_t[c][:, cols], in0=z_sb[c][:, cols], scalar=amp,
                                            in1=g2_sb[c][:, cols], op0=ALU.mult, op1=ALU.mult)
 
         def turn(c):
@@ -327,49 +316,53 @@ def tile_time2vec_t_v_kernel(tc, x, W, P_vec, w, p_sc, sine_w, cosine_w, z, grad
                     mm_dx(go, 2, "acc0")
             if has_w:
                 mm_dw(i - 2, 0)
-            if has_c:
-                make_dz(i, 0)
             if has_n:
                 reduce_k(i + 1, 0)
+            if has_c:
+                make_dz(i, 0)
             if has_o:
                 out_dx(go, 1)
                 if go < G - 1:
                     mm_dx(go, 3, "acc0")
             if has_w:
                 mm_dw(i - 2, 1)
-            if has_c:
-                make_dz(i, 1)
-                interleave(i)
-                turn(i)
-            if has_q:
-                quantize_f(i - 1)
-            if has_o:
-                out_dx(go, 2)
-            if starts_dx:
-                mm_dx(i - 1 - G, 0, "acc0")
-            if has_w:
-                mm_dw(i - 2, 2)
             if has_n:
                 reduce_k(i + 1, 1)
                 reduce_r(i + 1, 0)
                 sine(i + 1, 0)
+            if has_o:
+                out_dx(go, 2)
+            if has_w:
+                mm_dw(i - 2, 2)
+            if has_c:
+                make_dz(i, 1)
+                turn(i)
+                interleave(i)
+            if has_q:
+                quantize_f(i - 1)
+            if starts_dx:
+                mm_dx(i - 1 - G, 0, "acc0")
             if has_o:
                 out_dx(go, 3)
             if starts_dx:
                 mm_dx(i - 1 - G, 1, "acc0")
             if has_w:
                 mm_dw(i - 2, 3)
-            if has_q:
-                quantize_t(i - 1)
             if has_n:
                 reduce_r(i + 1, 1)
                 sine(i + 1, 1)
+            if has_q:
+                quantize_t(i - 1)
             if has_c:
                 gather(i)
             if has_w and (i - 2) % G == G - 1:
                 out_dw((i - 2) // G)
-            if i == 0 or i == 1:
-                w_quantize(i)
+            if i == 0:
+                x_quantize(3)
+            if i == 1 or i == 2:
+                w_turn(i - 1)
+            if i == 2 or i == 3:
+                w_quantize(i - 2)
 
         def last_but_one_step():
             out_dx(G - 2, 0)

@@ -62,9 +62,11 @@ def tile_time2vec_t_v_kernel(tc, x, W, P_vec, w, p_sc, sine_w, cosine_w, z, grad
 
         x_sb = {}
 
-        def load_x(g):
+        def load_x(g, pieces):
             xt = keep.tile([P, J, PASS], BF16, name="x%d" % g, tag="x%d" % g)
-            nc.sync.dma_start(out=xt[:], in_=x_v[g])
+            width = PASS // pieces
+            for k in range(pieces):
+                nc.sync.dma_start(out=xt[:, :, k * width:(k + 1) * width], in_=x_v[g][:, :, k * width:(k + 1) * width])
             x_sb[g] = xt
 
         z_sb = {}
@@ -86,11 +88,11 @@ def tile_time2vec_t_v_kernel(tc, x, W, P_vec, w, p_sc, sine_w, cosine_w, z, grad
             nc.sync.dma_start(out=gt[:], in_=go_v[g][:, :, 0:PASS])
             g1_sb[g] = gt
 
-        load_x(0)
-        load_x(1)
-        load_x(2)
+        load_x(0, 2)
+        load_x(1, 1)
+        load_x(2, 1)
         load_chunk(0)
-        load_x(3)
+        load_x(3, 1)
         w_sb = keep.tile([P, 4, 2 * PASS], BF16, name="w_sb", tag="w_sb")
         nc.sync.dma_start(out=w_sb[:], in_=w_v)
         load_chunk(1)
@@ -100,9 +102,13 @@ def tile_time2vec_t_v_kernel(tc, x, W, P_vec, w, p_sc, sine_w, cosine_w, z, grad
         xs = keep.tile([P, G, PASS], U8, name="xs", tag="xs", align_bytes=64)
         xg_t = {}
 
-        def x_interleave(g, engine_copy):
-            xg_t[g] = stream.tile([P, PASS, J], BF16, name="xg%d" % g, tag="xg", bufs=2, align_bytes=64)
-            engine_copy(out=xg_t[g][:], in_=x_sb[g][:].rearrange("p j f -> p f j"))
+        def interleaved(engine_copy, dst, src):
+            engine_copy(out=dst.rearrange("p (c i) j -> p c j i", i=4), in_=src.rearrange("p j (c i) -> p c j i", i=4))
+
+        def x_interleave(g, engine_copy, lo=0, hi=PASS):
+            if lo == 0:
+                xg_t[g] = stream.tile([P, PASS, J], BF16, name="xg%d" % g, tag="xg", bufs=2, align_bytes=64)
+            interleaved(engine_copy, xg_t[g][:, lo:hi, :], x_sb[g][:, :, lo:hi])
 
         def x_quantize(g):
             nc.vector.quantize_mx(out=xc[:, g, :].bitcast(E4), scales=xs[:, g, :],
@@ -128,7 +134,8 @@ def tile_time2vec_t_v_kernel(tc, x, W, P_vec, w, p_sc, sine_w, cosine_w, z, grad
         pr2 = fma("pr2", sw_2f, cw_f)
         ncw = fma("ncw", cwb[:], -1.0)
 
-        x_interleave(0, nc.vector.tensor_copy)
+        x_interleave(0, nc.vector.tensor_copy, 0, 256)
+        x_interleave(0, nc.vector.tensor_copy, 256, PASS)
         n2c = small("n2c")
         nc.vector.tensor_scalar_max(out=n2c[:], in0=n2, scalar1=1e-30)
         t2 = small("t2")
@@ -245,7 +252,7 @@ def tile_time2vec_t_v_kernel(tc, x, W, P_vec, w, p_sc, sine_w, cosine_w, z, grad
 
         def interleave(c):
             dzg = stream.tile([P, PASS, J], BF16, name="dzg%d" % c, tag="dzg", bufs=2, align_bytes=64)
-            nc.scalar.copy(out=dzg[:], in_=dz_t[c][:].rearrange("p (j f) -> p f j", j=J))
+            interleaved(nc.scalar.copy, dzg[:], dz_t[c][:].rearrange("p (j f) -> p j f", j=J))
             dzg_t[c] = dzg
 
         def gather(c):

@@ -73,10 +73,13 @@ def tile_time2vec_t_v_kernel(tc, x, W, P_vec, w, p_sc, sine_w, cosine_w, z, grad
         g2_sb = {}
         g1_sb = {}
 
-        def load_chunk(c):
+        def load_chunk(c, pieces=1):
             h, g = divmod(c, G)
             zt = stream.tile([P, J * PASS], F32, name="z%d" % c, tag="z", bufs=4)
-            nc.sync.dma_start(out=zt[:].rearrange("p (j f) -> p j f", j=J), in_=z_v[g][:, :, h * PASS:(h + 1) * PASS])
+            rows = J // pieces
+            for k in range(pieces):
+                nc.sync.dma_start(out=zt[:].rearrange("p (j f) -> p j f", j=J)[:, k * rows:(k + 1) * rows, :],
+                                  in_=z_v[g][:, k * rows:(k + 1) * rows, h * PASS:(h + 1) * PASS])
             gt = stream.tile([P, J * PASS], BF16, name="g2_%d" % c, tag="g2", bufs=4)
             nc.sync.dma_start(out=gt[:].rearrange("p (j f) -> p j f", j=J),
                               in_=go_v[g][:, :, PASS * (1 + h):PASS * (2 + h)])
@@ -91,12 +94,12 @@ def tile_time2vec_t_v_kernel(tc, x, W, P_vec, w, p_sc, sine_w, cosine_w, z, grad
         load_x(0, 2)
         load_x(1, 1)
         load_x(2, 1)
-        load_chunk(0)
+        load_chunk(0, 2)
+        load_chunk(1)
         load_x(3, 1)
+        load_chunk(2)
         w_sb = keep.tile([P, 4, 2 * PASS], BF16, name="w_sb", tag="w_sb")
         nc.sync.dma_start(out=w_sb[:], in_=w_v)
-        load_chunk(1)
-        load_chunk(2)
 
         xc = keep.tile([P, G, PASS], U32, name="xc", tag="xc", align_bytes=64)
         xs = keep.tile([P, G, PASS], U8, name="xs", tag="xs", align_bytes=64)
@@ -124,45 +127,49 @@ def tile_time2vec_t_v_kernel(tc, x, W, P_vec, w, p_sc, sine_w, cosine_w, z, grad
 
         halfpi = small("halfpi")
         nc.vector.tensor_scalar(out=halfpi[:], in0=warm[:], scalar1=0.0, scalar2=0.5 * PI, op0=ALU.mult, op1=ALU.add)
-        sw_f = fma("sw_f", swb[:], 1.0)
-        sw_2f = fma("sw_2f", swb[:], 2.0)
-        cw_f = fma("cw_f", cwb[:], 1.0)
-        sw2 = fma("sw2", sw_f, sw_f)
-        cw2 = fma("cw2", cw_f, cw_f)
-        n2 = fma("n2", sw2, 1.0, cw2)
-        df = fma("df", sw2, -1.0, cw2)
-        pr2 = fma("pr2", sw_2f, cw_f)
-        ncw = fma("ncw", cwb[:], -1.0)
-
+        sw2 = small("sw2")
+        nc.vector.tensor_tensor(out=sw2[:], in0=swb[:], in1=swb[:], op=ALU.mult)
+        cw2 = small("cw2")
+        nc.vector.tensor_tensor(out=cw2[:], in0=cwb[:], in1=cwb[:], op=ALU.mult)
+        n2 = small("n2")
+        nc.vector.scalar_tensor_tensor(out=n2[:], in0=sw2[:], scalar=1e-30, in1=cw2[:], op0=ALU.add, op1=ALU.add)
+        df = small("df")
+        nc.vector.tensor_tensor(out=df[:], in0=cw2[:], in1=sw2[:], op=ALU.subtract)
+        inv = small("inv")
+        nc.vector.reciprocal(out=inv[:], in_=n2[:])
+        t2 = small("t2")
+        nc.vector.tensor_scalar(out=t2[:], in0=df[:], scalar1=0.0, scalar2=-2.0, op0=ALU.is_ge, op1=ALU.mult)
         x_interleave(0, nc.vector.tensor_copy, 0, 256)
         x_interleave(0, nc.vector.tensor_copy, 256, PASS)
-        n2c = small("n2c")
-        nc.vector.tensor_scalar_max(out=n2c[:], in0=n2, scalar1=1e-30)
-        t2 = small("t2")
-        nc.vector.tensor_scalar(out=t2[:], in0=df, scalar1=0.0, scalar2=-2.0, op0=ALU.is_ge, op1=ALU.mult)
-        inv = small("inv")
-        nc.vector.reciprocal(out=inv[:], in_=n2c[:])
         x_interleave(1, nc.vector.tensor_copy)
 
+        sw_2f = fma("sw_2f", swb[:], 2.0)
+        cw_f = fma("cw_f", cwb[:], 1.0)
+        pr2 = fma("pr2", sw_2f, cw_f)
         q1 = fma("q1", t2[:], inv[:], inv[:])
         pair = small("pair", 2)
         s2 = fma("", pr2, q1, None, pair[:, 0:1])
         fma("", pr2, q1, halfpi[:], pair[:, 1:2])
-        nc2 = fma("nc2", df, q1)
+        nc2 = fma("nc2", df[:], q1)
 
         sc0 = small("sc0", 2)
         nc.scalar.activation(out=sc0[:], in_=pair[:], func=ACT.Sin)
         off = fma("off", t2[:], 0.25 * PI, halfpi[:])
         part0 = fma("part0", sc0[:, 1:2], s2)
         offp = fma("offp", s2, 0.5, off)
-        moved = fma("moved0", sc0[:, 0:1], nc2, part0)
+        moved0 = fma("moved0", sc0[:, 0:1], nc2, part0)
         offt = fma("offt", offp, 1.0 / TWO_PI)
+        sc1 = small("sc1", 2)
+        nc.scalar.activation(out=sc1[:], in_=pair[:], func=ACT.Sin, scale=1.0, bias=moved0)
         hp = fma("hp", offp, -1.0, halfpi[:])
-        for it in (1, 2):
-            sc = small("sc%d" % it, 2)
-            nc.scalar.activation(out=sc[:], in_=pair[:], func=ACT.Sin, scale=1.0, bias=moved)
-            part = fma("part%d" % it, sc[:, 1:2], s2, moved)
-            moved = fma("moved%d" % it, sc[:, 0:1], nc2, part)
+        part1 = fma("part1", sc1[:, 1:2], s2, moved0)
+        sw_f = fma("sw_f", swb[:], 1.0)
+        moved1 = fma("moved1", sc1[:, 0:1], nc2, part1)
+        ncw = fma("ncw", cwb[:], -1.0)
+        sc2 = small("sc2", 2)
+        nc.scalar.activation(out=sc2[:], in_=pair[:], func=ACT.Sin, scale=1.0, bias=moved1)
+        part2 = fma("part2", sc2[:, 1:2], s2, moved1)
+        moved = fma("moved2", sc2[:, 0:1], nc2, part2)
         turns = fma("turns", moved, 0.5 / TWO_PI, offt)
         phi = fma("phi", moved, 0.5, offp)
         sin_phi = small("sin_phi")
@@ -178,7 +185,6 @@ def tile_time2vec_t_v_kernel(tc, x, W, P_vec, w, p_sc, sine_w, cosine_w, z, grad
         wf = small("wf")
         nc.vector.tensor_copy(out=wf[:], in_=wb[:])
         x_quantize(2)
-        x_interleave(3, nc.scalar.copy)
 
         wc = keep.tile([P, H, PASS], U32, name="wc", tag="wc", align_bytes=64)
         ws = keep.tile([P, H, PASS], U8, name="ws", tag="ws", align_bytes=64)
@@ -365,6 +371,8 @@ def tile_time2vec_t_v_kernel(tc, x, W, P_vec, w, p_sc, sine_w, cosine_w, z, grad
             if has_w and (i - 2) % G == G - 1:
                 out_dw((i - 2) // G)
             if i == 0:
+                x_interleave(3, nc.scalar.copy)
+            if i == 1:
                 x_quantize(3)
             if i == 1 or i == 2:
                 w_turn(i - 1)

from contextlib import ExitStack

import concourse.mybir as mybir
from concourse.masks import make_identity

FLOPS = 2 * 2 * 2048 * 1024 * 512

F32 = mybir.dt.float32
BF16 = mybir.dt.bfloat16
I32 = mybir.dt.int32
U32 = mybir.dt.uint32
U8 = mybir.dt.uint8
E4 = mybir.dt.float8_e4m3fn_x4
E5 = mybir.dt.float8_e5m2_x4
ALU = mybir.AluOpType
ACT = mybir.ActivationFunctionType

P = 128
J = 4
PASS = 512
G = 4
H = 2
NCH = G * H
HALF = 1024
PI = 3.141592653589793
TWO_PI = 2.0 * PI


def tile_time2vec_t_v_kernel(tc, x, W, P_vec, w, p_sc, sine_w, cosine_w, z, grad_out, out_0, out_1):
    nc = tc.nc

    z_v = z.rearrange("(g p j) f -> g p j f", p=P, j=J)
    go_v = grad_out.rearrange("(g p j) c -> g p j c", p=P, j=J)
    x_v = x.rearrange("(g p j) f -> g p j f", p=P, j=J)
    w_v = W.rearrange("(a p) n -> p a n", p=P)
    o0_v = out_0.rearrange("(g p j) k -> g p j k", p=P, j=J)

    with ExitStack() as ctx:
        const = ctx.enter_context(tc.tile_pool(name="const", bufs=1))
        keep = ctx.enter_context(tc.tile_pool(name="keep", bufs=1))
        stream = ctx.enter_context(tc.tile_pool(name="stream", bufs=2))
        psum = ctx.enter_context(tc.psum_pool(name="psum", bufs=1))
        ctx.enter_context(tc.manual_schedule())

        def small(name, cols=1, dtype=F32):
            return const.tile([P, cols], dtype, name=name, tag=name)

        swb = small("swb", 1, BF16)
        cwb = small("cwb", 1, BF16)
        wb = small("wb", 1, BF16)
        with nc.allow_non_contiguous_dma(reason="one scalar spread over the partitions"):
            nc.sync.dma_start(out=swb[:], in_=sine_w.partition_broadcast(P))
            nc.scalar.dma_start(out=cwb[:], in_=cosine_w.partition_broadcast(P))
            nc.gpsimd.dma_start(out=wb[:], in_=w.partition_broadcast(P))

        warm = small("warm")
        nc.vector.memset(warm[:], 0.0)
        warm2 = small("warm2")
        nc.scalar.activation(out=warm2[:], in_=warm[:], func=ACT.Sin)
        ident = const.tile([P, P], F32, name="ident", tag="ident")
        make_identity(nc, ident[:])

        x_sb = {}

        def load_x(g, pieces):
            xt = keep.tile([P, J, PASS], BF16, name="x%d" % g, tag="x%d" % g)
            width = PASS // pieces
            for k in range(pieces):
                nc.sync.dma_start(out=xt[:, :, k * width:(k + 1) * width], in_=x_v[g][:, :, k * width:(k + 1) * width])
            x_sb[g] = xt

        z_sb = {}
        g2_sb = {}
        g1_sb = {}

        def load_chunk(c, pieces=1):
            h, g = divmod(c, G)
            zt = stream.tile([P, J * PASS], F32, name="z%d" % c, tag="z", bufs=4)
            rows = J // pieces
            for k in range(pieces):
                nc.sync.dma_start(out=zt[:].rearrange("p (j f) -> p j f", j=J)[:, k * rows:(k + 1) * rows, :],
                                  in_=z_v[g][:, k * rows:(k + 1) * rows, h * PASS:(h + 1) * PASS])
            gt = stream.tile([P, J * PASS], BF16, name="g2_%d" % c, tag="g2", bufs=4)
            nc.sync.dma_start(out=gt[:].rearrange("p (j f) -> p j f", j=J),
                              in_=go_v[g][:, :, PASS * (1 + h):PASS * (2 + h)])
            z_sb[c] = zt
            g2_sb[c] = gt

        def load_g1(g):
            gt = keep.tile([P, J, PASS], BF16, name="g1_%d" % g, tag="g1_%d" % g)
            nc.sync.dma_start(out=gt[:], in_=go_v[g][:, :, 0:PASS])
            g1_sb[g] = gt

        load_x(0, 2)
        load_x(1, 1)
        load_x(2, 1)
        load_chunk(0, 2)
        load_chunk(1)
        load_x(3, 1)
        load_chunk(2)
        w_sb = keep.tile([P, 4, 2 * PASS], BF16, name="w_sb", tag="w_sb")
        nc.sync.dma_start(out=w_sb[:], in_=w_v)

        xc = keep.tile([P, G, PASS], U32, name="xc", tag="xc", align_bytes=64)
        xs = keep.tile([P, G, PASS], U8, name="xs", tag="xs", align_bytes=64)
        xg_t = {}

        def interleaved(engine_copy, dst, src):
            engine_copy(out=dst.rearrange("p (c i) j -> p c j i", i=4), in_=src.rearrange("p j (c i) -> p c j i", i=4))

        def x_interleave(g, engine_copy, lo=0, hi=PASS):
            if lo == 0:
                xg_t[g] = stream.tile([P, PASS, J], BF16, name="xg%d" % g, tag="xg", bufs=2, align_bytes=64)
            interleaved(engine_copy, xg_t[g][:, lo:hi, :], x_sb[g][:, :, lo:hi])

        def x_quantize(g):
            nc.vector.quantize_mx(out=xc[:, g, :].bitcast(E4), scales=xs[:, g, :],
                                  in_=xg_t[g][:].rearrange("p f j -> p (f j)"))

        def fma(name, in_, scale, bias=None, cols=None):
            out = cols if cols is not None else small(name)[:]
            if bias is None:
                nc.scalar.activation(out=out, in_=in_, func=ACT.Copy, scale=scale)
            else:
                nc.scalar.activation(out=out, in_=in_, func=ACT.Identity, scale=scale, bias=bias)
            return out

        halfpi = small("halfpi")
        nc.vector.tensor_scalar(out=halfpi[:], in0=warm[:], scalar1=0.0, scalar2=0.5 * PI, op0=ALU.mult, op1=ALU.add)
        sw2 = small("sw2")
        nc.vector.tensor_tensor(out=sw2[:], in0=swb[:], in1=swb[:], op=ALU.mult)
        cw2 = small("cw2")
        nc.vector.tensor_tensor(out=cw2[:], in0=cwb[:], in1=cwb[:], op=ALU.mult)
        n2 = small("n2")
        nc.vector.scalar_tensor_tensor(out=n2[:], in0=sw2[:], scalar=1e-30, in1=cw2[:], op0=ALU.add, op1=ALU.add)
        df = small("df")
        nc.vector.tensor_tensor(out=df[:], in0=cw2[:], in1=sw2[:], op=ALU.subtract)
        inv = small("inv")
        nc.vector.reciprocal(out=inv[:], in_=n2[:])
        t2 = small("t2")
        nc.vector.tensor_scalar(out=t2[:], in0=df[:], scalar1=0.0, scalar2=-2.0, op0=ALU.is_ge, op1=ALU.mult)
        x_interleave(0, nc.vector.tensor_copy, 0, 256)
        x_interleave(0, nc.vector.tensor_copy, 256, PASS)
        x_interleave(1, nc.vector.tensor_copy)

        sw_2f = fma("sw_2f", swb[:], 2.0)
        cw_f = fma("cw_f", cwb[:], 1.0)
        pr2 = fma("pr2", sw_2f, cw_f)
        q1 = fma("q1", t2[:], inv[:], inv[:])
        pair = small("pair", 2)
        s2 = fma("", pr2, q1, None, pair[:, 0:1])
        fma("", pr2, q1, halfpi[:], pair[:, 1:2])
        nc2 = fma("nc2", df[:], q1)

        sc0 = small("sc0", 2)
        nc.scalar.activation(out=sc0[:], in_=pair[:], func=ACT.Sin)
        off = fma("off", t2[:], 0.25 * PI, halfpi[:])
        part0 = fma("part0", sc0[:, 1:2], s2)
        offp = fma("offp", s2, 0.5, off)
        moved0 = fma("moved0", sc0[:, 0:1], nc2, part0)
        offt = fma("offt", offp, 1.0 / TWO_PI)
        sc1 = small("sc1", 2)
        nc.scalar.activation(out=sc1[:], in_=pair[:], func=ACT.Sin, scale=1.0, bias=moved0)
        hp = fma("hp", offp, -1.0, halfpi[:])
        part1 = fma("part1", sc1[:, 1:2], s2, moved0)
        sw_f = fma("sw_f", swb[:], 1.0)
        moved1 = fma("moved1", sc1[:, 0:1], nc2, part1)
        ncw = fma("ncw", cwb[:], -1.0)
        sc2 = small("sc2", 2)
        nc.scalar.activation(out=sc2[:], in_=pair[:], func=ACT.Sin, scale=1.0, bias=moved1)
        part2 = fma("part2", sc2[:, 1:2], s2, moved1)
        moved = fma("moved2", sc2[:, 0:1], nc2, part2)
        turns = fma("turns", moved, 0.5 / TWO_PI, offt)
        phi = fma("phi", moved, 0.5, offp)
        sin_phi = small("sin_phi")
        nc.scalar.activation(out=sin_phi[:], in_=phi, func=ACT.Sin)
        cos_phi = small("cos_phi")
        nc.scalar.activation(out=cos_phi[:], in_=moved, func=ACT.Sin, scale=-0.5, bias=hp)
        m2 = fma("m2", sin_phi[:], sw_f)
        amp = fma("amp", cos_phi[:], ncw, m2)

        x_quantize(0)
        x_interleave(2, nc.vector.tensor_copy)
        x_quantize(1)
        wf = small("wf")
        nc.vector.tensor_copy(out=wf[:], in_=wb[:])
        x_quantize(2)

        wc = keep.tile([P, H, PASS], U32, name="wc", tag="wc", align_bytes=64)
        ws = keep.tile([P, H, PASS], U8, name="ws", tag="ws", align_bytes=64)
        w_words = w_sb[:].rearrange("p a n -> p (a n)").bitcast(F32)
        wg_t = {}

        def w_turn(h):
            wg = stream.tile([P, PASS, J], BF16, name="wg%d" % h, tag="wg", bufs=2, align_bytes=64)
            wg_words = wg[:].rearrange("q c t -> q (c t)").bitcast(F32)
            wg_t[h] = wg
            for ap in range(2):
                tp = psum.tile([P, 2, 2, P], F32, name="tpw%d%d" % (h, ap), tag="tp", bufs=2)
                for l in range(2):
                    base = (2 * ap + l) * PASS + 256 * h
                    for u in range(2):
                        nc.tensor.transpose(tp[:, l, u, :], w_words[:, base + u:base + 256:2], ident[:])
                nc.scalar.copy(
                    out=wg_words[:, ap * PASS:(ap + 1) * PASS].rearrange("q (l p u) -> q l p u", l=2, u=2),
                    in_=tp[:].rearrange("q l u p -> q l p u"))

        def w_quantize(h):
            nc.vector.quantize_mx(out=wc[:, h, :].bitcast(E4), scales=ws[:, h, :],
                                  in_=wg_t[h][:].rearrange("q c t -> q (c t)"))

        fc = keep.tile([P, NCH, PASS], U32, name="fc", tag="fc", align_bytes=64)
        fs = keep.tile([P, NCH, PASS], U8, name="fs", tag="fs", align_bytes=64)
        k_t = {}
        dz_t = {}
        dzg_t = {}
        fg_t = {}
        tp_t = {}
        tc_t = {}
        ts_t = {}
        acc1 = {}
        acc0 = {}

        def reduce_k(c, a):
            if a == 0:
                k_t[c] = stream.tile([P, J * PASS], I32, name="k%d" % c, tag="k", bufs=2)
            cols = slice(a * HALF, (a + 1) * HALF)
            nc.vector.tensor_scalar(out=k_t[c][:, cols], in0=z_sb[c][:, cols], scalar1=1.0 / TWO_PI,
                                    scalar2=turns, op0=ALU.mult, op1=ALU.add)

        def reduce_r(c, a):
            cols = slice(a * HALF, (a + 1) * HALF)
            nc.vector.scalar_tensor_tensor(out=z_sb[c][:, cols], in0=k_t[c][:, cols], scalar=-TWO_PI,
                                           in1=z_sb[c][:, cols], op0=ALU.mult, op1=ALU.add)

        def sine(c, a):
            cols = slice(a * HALF, (a + 1) * HALF)
            nc.scalar.activation(out=z_sb[c][:, cols], in_=z_sb[c][:, cols], func=ACT.Sin, bias=phi, scale=1.0)

        def make_dz(c, a):
            if a == 0:
                dz_t[c] = stream.tile([P, J * PASS], BF16, name="dz%d" % c, tag="dz", bufs=3)
            cols = slice(a * HALF, (a + 1) * HALF)
            nc.vector.scalar_tensor_tensor(out=dz_t[c][:, cols], in0=z_sb[c][:, cols], scalar=amp,
                                           in1=g2_sb[c][:, cols], op0=ALU.mult, op1=ALU.mult)

        def turn(c):
            words = dz_t[c][:].bitcast(F32)
            tps = []
            for jp in range(2):
                tp = psum.tile([P, 2, 2, P], F32, name="tp%d_%d" % (c, jp), tag="tp", bufs=2)
                for l in range(2):
                    base = (2 * jp + l) * 256
                    for u in range(2):
                        nc.tensor.transpose(tp[:, l, u, :], words[:, base + u:base + 256:2], ident[:])
                tps.append(tp)
            tp_t[c] = tps

        def interleave(c):
            dzg = stream.tile([P, PASS, J], BF16, name="dzg%d" % c, tag="dzg", bufs=2, align_bytes=64)
            interleaved(nc.scalar.copy, dzg[:], dz_t[c][:].rearrange("p (j f) -> p j f", j=J))
            dzg_t[c] = dzg

        def gather(c):
            fg = stream.tile([P, PASS, J], BF16, name="fg%d" % c, tag="fg", bufs=2, align_bytes=64)
            fg_words = fg[:].rearrange("q c t -> q (c t)").bitcast(F32)
            for jp in range(2):
                nc.scalar.copy(
                    out=fg_words[:, jp * PASS:(jp + 1) * PASS].rearrange("q (l p u) -> q l p u", l=2, u=2),
                    in_=tp_t[c][jp][:].rearrange("q l u p -> q l p u"))
            fg_t[c] = fg

        def quantize_f(c):
            nc.vector.quantize_mx(out=fc[:, c, :].bitcast(E5), scales=fs[:, c, :],
                                  in_=fg_t[c][:].rearrange("q c t -> q (c t)"))

        def quantize_t(c):
            tcod = stream.tile([P, PASS], U32, name="tc%d" % c, tag="tcod", bufs=3, align_bytes=64)
            tsc = stream.tile([P, PASS], U8, name="ts%d" % c, tag="tsc", bufs=3, align_bytes=64)
            nc.vector.quantize_mx(out=tcod[:].bitcast(E5), scales=tsc[:],
                                  in_=dzg_t[c][:].rearrange("p f j -> p (f j)"))
            tc_t[c] = tcod
            ts_t[c] = tsc

        def mm_dw(c, m):
            h, g = divmod(c, G)
            if g == 0:
                acc1[m] = psum.tile([P, PASS], F32, name="acc1_%d_%d" % (h, m), tag="acc1_%d" % m)
            cols = slice(m * P, (m + 1) * P)
            nc.tensor.matmul_mx(out=acc1[m][:], lhsT=xc[:, g, cols].bitcast(E4), lhsT_scale=xs[:, g, cols],
                                rhs=tc_t[c][:].bitcast(E5), rhs_scale=ts_t[c][:],
                                start=(g == 0), stop=(g == G - 1))

        def mm_dx(g, j, tag):
            acc = psum.tile([P, PASS], F32, name="acc0_%d_%d" % (g, j), tag=tag, bufs=2)
            cols = slice(j * P, (j + 1) * P)
            for h in range(H):
                nc.tensor.matmul_mx(out=acc[:], lhsT=fc[:, h * G + g, cols].bitcast(E5),
                                    lhsT_scale=fs[:, h * G + g, cols],
                                    rhs=wc[:, h, :].bitcast(E4), rhs_scale=ws[:, h, :],
                                    start=(h == 0), stop=(h == H - 1))
            acc0[(g, j)] = acc

        def out_dx(g, j):
            o0 = stream.tile([P, PASS], F32, name="o0_%d_%d" % (g, j), tag="o0", bufs=8)
            nc.vector.scalar_tensor_tensor(out=o0[:], in0=g1_sb[g][:, j, :], scalar=wf[:, 0:1],
                                           in1=acc0[(g, j)][:], op0=ALU.mult, op1=ALU.add)
            nc.sync.dma_start(out=o0_v[g][:, j, :], in_=o0[:])

        def out_dw(h):
            for m in range(4):
                o1 = stream.tile([P, PASS], F32, name="o1_%d_%d" % (h, m), tag="o1", bufs=4)
                nc.scalar.copy(out=o1[:], in_=acc1[m][:])
                nc.scalar.dma_start(out=out_1[m * P:(m + 1) * P, h * PASS:(h + 1) * PASS], in_=o1[:])

        LAST = NCH - 1

        def step(i):
            has_n = 0 <= i + 1 < NCH
            has_c = 0 <= i < NCH
            has_q = 0 <= i - 1 < NCH
            has_w = 0 <= i - 2 < LAST
            has_o = G <= i - 2 < NCH
            starts_dx = has_q and i - 1 >= G
            go = i - 2 - G
            if has_o:
                out_dx(go, 0)
                if go < G - 1:
                    mm_dx(go, 2, "acc0")
            if has_w:
                mm_dw(i - 2, 0)
            if has_n:
                reduce_k(i + 1, 0)
            if has_c:
                make_dz(i, 0)
            if has_o:
                out_dx(go, 1)
                if go < G - 1:
                    mm_dx(go, 3, "acc0")
            if has_w:
                mm_dw(i - 2, 1)
            if has_n:
                reduce_k(i + 1, 1)
                reduce_r(i + 1, 0)
                sine(i + 1, 0)
            if has_o:
                out_dx(go, 2)
            if has_w:
                mm_dw(i - 2, 2)
            if has_c:
                make_dz(i, 1)
                turn(i)
                interleave(i)
            if has_q:
                quantize_f(i - 1)
            if starts_dx:
                mm_dx(i - 1 - G, 0, "acc0")
            if has_o:
                out_dx(go, 3)
            if starts_dx:
                mm_dx(i - 1 - G, 1, "acc0")
            if has_w:
                mm_dw(i - 2, 3)
            if has_n:
                reduce_r(i + 1, 1)
                sine(i + 1, 1)
            if has_q:
                quantize_t(i - 1)
            if has_c:
                gather(i)
            if has_w and (i - 2) % G == G - 1:
                out_dw((i - 2) // G)
            if i == 0:
                x_interleave(3, nc.scalar.copy)
            if i == 1:
                x_quantize(3)
            if i == 1 or i == 2:
                w_turn(i - 1)
            if i == 2 or i == 3:
                w_quantize(i - 2)

        def last_but_one_step():
            out_dx(G - 2, 0)
            mm_dx(G - 2, 2, "acc0")
            for m in range(4):
                mm_dw(LAST - 1, m)
            out_dx(G - 2, 1)
            mm_dx(G - 2, 3, "acc0")
            quantize_t(LAST)
            for m in range(4):
                mm_dw(LAST, m)
            out_dw(H - 1)
            quantize_f(LAST)
            mm_dx(G - 1, 0, "tp")
            mm_dx(G - 1, 1, "tp")
            out_dx(G - 2, 2)
            mm_dx(G - 1, 2, "acc0")
            out_dx(G - 2, 3)
            mm_dx(G - 1, 3, "acc0")

        for i in range(-1, NCH + 2):
            if 3 <= i + 3 < NCH:
                load_chunk(i + 3)
            if 2 <= i < 2 + G:
                load_g1(i - 2)
            if i == NCH:
                last_but_one_step()
            else:
                step(i)
